import numpy as np
import ml_dtypes

BF16 = ml_dtypes.bfloat16


def bf(x):
    return np.asarray(x, np.float32).astype(BF16)


def f32(x):
    return np.asarray(x, np.float32)


def f64(x):
    return np.asarray(x).astype(np.float64)


def striped(idx):
    return np.tile(idx.reshape(-1, 16).T, (8, 1))


C, S, K, N = 512, 1024, 2, 2048


def setup_inputs():
    return {"support": f32(np.random.standard_normal((C, N))), "attended": bf(np.random.standard_normal((C, S))), "wo": bf(np.random.standard_normal((C, C)) / np.sqrt(C)), "bo": f32(0.1 * np.random.standard_normal((C, 1))), "offs": striped(np.concatenate([np.random.permutation(S) for _ in range(K)]))}


def reference(support, attended, wo, bo, offs):
    idx = offs[:16].T.reshape(-1)
    refined = f64(wo).T @ f64(attended) + f64(bo)
    return f64(support) + refined[:, idx]

@@ -1,0 +1,70 @@
+import concourse.mybir as mybir
+
+P = 128
+C, S, N = 512, 1024, 2048
+BLOCKS = C // P
+BANK = 512
+HALVES = S // BANK
+PIECES = N // S
+PIECE_COLS = S // 16
+
+FLOPS = 2 * C * C * S
+
+BF16, F32, U16 = mybir.dt.bfloat16, mybir.dt.float32, mybir.dt.uint16
+ADD = mybir.AluOpType.add
+IDENTITY = mybir.ActivationFunctionType.Identity
+
+
+def tile_entityguidedcrossattention_kernel(tc, support, attended, wo, bo, offs, out):
+    nc = tc.nc
+    with (
+        tc.tile_pool(name="held", bufs=1) as held,
+        tc.psum_pool(name="psum", bufs=2) as psum,
+    ):
+        offsets = held.tile([P, N // 16], U16, name="offsets")
+        nc.sync.dma_start(offsets[:], offs)
+
+        bias = held.tile([P, BLOCKS], F32, name="bias")
+        with nc.allow_non_contiguous_dma(reason="512 bias values, one to a partition"):
+            nc.scalar.dma_start(bias[:], bo.rearrange("(b p) o -> p (b o)", p=P))
+
+        weights, classes = [], []
+        for db in range(BLOCKS):
+            rows = slice(db * P, (db + 1) * P)
+            w = held.tile([P, C], BF16, name=f"weights{db}")
+            nc.scalar.dma_start(w[:], wo[rows, :])
+            weights.append(w)
+            a = held.tile([P, S], BF16, name=f"classes{db}")
+            nc.sync.dma_start(a[:], attended[rows, :])
+            classes.append(a)
+
+        samples = {}
+        for cb in range(BLOCKS):
+            for k in range(PIECES):
+                t = held.tile([P, S], F32, name=f"samples{cb}_{k}")
+                queue = nc.sync if k == 0 else nc.scalar
+                queue.dma_start(t[:], support[cb * P : (cb + 1) * P, k * S : (k + 1) * S])
+                samples[cb, k] = t
+
+        for cb in range(BLOCKS):
+            refined = held.tile([P, S], F32, name=f"refined{cb}")
+            banks = [psum.tile([P, BANK], F32, name=f"bank{h}") for h in range(HALVES)]
+            for db in range(BLOCKS):
+                for h in range(HALVES):
+                    nc.tensor.matmul(
+                        banks[h][:],
+                        weights[db][:, cb * P : (cb + 1) * P],
+                        classes[db][:, h * BANK : (h + 1) * BANK],
+                        start=(db == 0),
+                        stop=(db == BLOCKS - 1),
+                    )
+            for h in range(HALVES):
+                nc.scalar.activation(
+                    refined[:, h * BANK : (h + 1) * BANK], banks[h][:], IDENTITY, bias=bias[:, cb : cb + 1]
+                )
+
+            for k in range(PIECES):
+                summed = held.tile([P, S], F32, name=f"summed{cb}_{k}")
+                picked = refined[:].indirect(offsets[:, k * PIECE_COLS : (k + 1) * PIECE_COLS])
+                nc.vector.tensor_tensor(summed[:], picked, samples[cb, k][:], ADD)
+                nc.sync.dma_start(out[cb * P : (cb + 1) * P, k * S : (k + 1) * S], summed[:])

@@ -17,54 +17,56 @@ IDENTITY = mybir.ActivationFunctionType.Identity
 
 def tile_entityguidedcrossattention_kernel(tc, support, attended, wo, bo, offs, out):
     nc = tc.nc
+    wo_blocks = wo.rearrange("(b p) c -> p b c", p=P)
     with (
         tc.tile_pool(name="held", bufs=1) as held,
-        tc.psum_pool(name="psum", bufs=2) as psum,
+        tc.psum_pool(name="psum", bufs=4) as psum,
     ):
-        offsets = held.tile([P, N // 16], U16, name="offsets")
-        nc.sync.dma_start(offsets[:], offs)
-
         bias = held.tile([P, BLOCKS], F32, name="bias")
         with nc.allow_non_contiguous_dma(reason="512 bias values, one to a partition"):
             nc.scalar.dma_start(bias[:], bo.rearrange("(b p) o -> p (b o)", p=P))
 
-        weights, classes = [], []
-        for db in range(BLOCKS):
-            rows = slice(db * P, (db + 1) * P)
-            w = held.tile([P, C], BF16, name=f"weights{db}")
-            nc.scalar.dma_start(w[:], wo[rows, :])
-            weights.append(w)
-            a = held.tile([P, S], BF16, name=f"classes{db}")
-            nc.sync.dma_start(a[:], attended[rows, :])
-            classes.append(a)
+        def load_weights(cb):
+            w = held.tile([P, BLOCKS, P], BF16, name=f"weights{cb}")
+            nc.sync.dma_start(w[:], wo_blocks[:, :, cb * P : (cb + 1) * P])
+            return w
 
-        samples = {}
+        def load_samples(cb, k):
+            t = held.tile([P, S], F32, name=f"samples{cb}_{k}")
+            nc.sync.dma_start(t[:], support[cb * P : (cb + 1) * P, k * S : (k + 1) * S])
+            return t
+
+        weights = {0: load_weights(0)}
+        classes = {}
+        for h in range(HALVES):
+            for db in range(BLOCKS):
+                a = held.tile([P, BANK], BF16, name=f"classes{db}_{h}")
+                nc.sync.dma_start(a[:], attended[db * P : (db + 1) * P, h * BANK : (h + 1) * BANK])
+                classes[db, h] = a
+        offsets = held.tile([P, N // 16], U16, name="offsets")
+        nc.sync.dma_start(offsets[:], offs)
+        samples = {(0, 0): load_samples(0, 0)}
+        for cb in range(1, BLOCKS):
+            weights[cb] = load_weights(cb)
         for cb in range(BLOCKS):
             for k in range(PIECES):
-                t = held.tile([P, S], F32, name=f"samples{cb}_{k}")
-                queue = nc.sync if k == 0 else nc.scalar
-                queue.dma_start(t[:], support[cb * P : (cb + 1) * P, k * S : (k + 1) * S])
-                samples[cb, k] = t
+                if (cb, k) != (0, 0):
+                    samples[cb, k] = load_samples(cb, k)
 
         for cb in range(BLOCKS):
             refined = held.tile([P, S], F32, name=f"refined{cb}")
-            banks = [psum.tile([P, BANK], F32, name=f"bank{h}") for h in range(HALVES)]
-            for db in range(BLOCKS):
-                for h in range(HALVES):
-                    nc.tensor.matmul(
-                        banks[h][:],
-                        weights[db][:, cb * P : (cb + 1) * P],
-                        classes[db][:, h * BANK : (h + 1) * BANK],
-                        start=(db == 0),
-                        stop=(db == BLOCKS - 1),
-                    )
             for h in range(HALVES):
+                bank = psum.tile([P, BANK], F32, name="bank")
+                for db in range(BLOCKS):
+                    nc.tensor.matmul(
+                        bank[:], weights[cb][:, db, :], classes[db, h][:], start=(db == 0), stop=(db == BLOCKS - 1)
+                    )
                 nc.scalar.activation(
-                    refined[:, h * BANK : (h + 1) * BANK], banks[h][:], IDENTITY, bias=bias[:, cb : cb + 1]
+                    refined[:, h * BANK : (h + 1) * BANK], bank[:], IDENTITY, bias=bias[:, cb : cb + 1]
                 )
 
             for k in range(PIECES):
                 summed = held.tile([P, S], F32, name=f"summed{cb}_{k}")
                 picked = refined[:].indirect(offsets[:, k * PIECE_COLS : (k + 1) * PIECE_COLS])
                 nc.vector.tensor_tensor(summed[:], picked, samples[cb, k][:], ADD)
-                nc.sync.dma_start(out[cb * P : (cb + 1) * P, k * S : (k + 1) * S], summed[:])
+                nc.scalar.dma_start(out[cb * P : (cb + 1) * P, k * S : (k + 1) * S], summed[:])

@@ -20,34 +20,28 @@ def tile_entityguidedcrossattention_kernel(tc, support, attended, wo, bo, offs, 
     wo_blocks = wo.rearrange("(b p) c -> p b c", p=P)
     with (
         tc.tile_pool(name="held", bufs=1) as held,
-        tc.psum_pool(name="psum", bufs=4) as psum,
+        tc.psum_pool(name="psum", bufs=2) as psum,
     ):
         bias = held.tile([P, BLOCKS], F32, name="bias")
         with nc.allow_non_contiguous_dma(reason="512 bias values, one to a partition"):
             nc.scalar.dma_start(bias[:], bo.rearrange("(b p) o -> p (b o)", p=P))
-
-        def load_weights(cb):
-            w = held.tile([P, BLOCKS, P], BF16, name=f"weights{cb}")
-            nc.sync.dma_start(w[:], wo_blocks[:, :, cb * P : (cb + 1) * P])
-            return w
 
         def load_samples(cb, k):
             t = held.tile([P, S], F32, name=f"samples{cb}_{k}")
             nc.sync.dma_start(t[:], support[cb * P : (cb + 1) * P, k * S : (k + 1) * S])
             return t
 
-        weights = {0: load_weights(0)}
-        classes = {}
-        for h in range(HALVES):
-            for db in range(BLOCKS):
-                a = held.tile([P, BANK], BF16, name=f"classes{db}_{h}")
-                nc.sync.dma_start(a[:], attended[db * P : (db + 1) * P, h * BANK : (h + 1) * BANK])
-                classes[db, h] = a
+        weights = held.tile([P, BLOCKS, C], BF16, name="weights")
+        nc.sync.dma_start(weights[:, :, 0:P], wo_blocks[:, :, 0:P])
+        classes = []
+        for db in range(BLOCKS):
+            a = held.tile([P, S], BF16, name=f"classes{db}")
+            nc.sync.dma_start(a[:], attended[db * P : (db + 1) * P, :])
+            classes.append(a)
         offsets = held.tile([P, N // 16], U16, name="offsets")
         nc.sync.dma_start(offsets[:], offs)
         samples = {(0, 0): load_samples(0, 0)}
-        for cb in range(1, BLOCKS):
-            weights[cb] = load_weights(cb)
+        nc.sync.dma_start(weights[:, :, P:C], wo_blocks[:, :, P:C])
         for cb in range(BLOCKS):
             for k in range(PIECES):
                 if (cb, k) != (0, 0):
@@ -55,18 +49,23 @@ def tile_entityguidedcrossattention_kernel(tc, support, attended, wo, bo, offs, 
 
         for cb in range(BLOCKS):
             refined = held.tile([P, S], F32, name=f"refined{cb}")
-            for h in range(HALVES):
-                bank = psum.tile([P, BANK], F32, name="bank")
-                for db in range(BLOCKS):
+            banks = [psum.tile([P, BANK], F32, name=f"bank{h}") for h in range(HALVES)]
+            for db in range(BLOCKS):
+                for h in range(HALVES):
                     nc.tensor.matmul(
-                        bank[:], weights[cb][:, db, :], classes[db, h][:], start=(db == 0), stop=(db == BLOCKS - 1)
+                        banks[h][:],
+                        weights[:, db, cb * P : (cb + 1) * P],
+                        classes[db][:, h * BANK : (h + 1) * BANK],
+                        start=(db == 0),
+                        stop=(db == BLOCKS - 1),
                     )
+            for h in range(HALVES):
                 nc.scalar.activation(
-                    refined[:, h * BANK : (h + 1) * BANK], bank[:], IDENTITY, bias=bias[:, cb : cb + 1]
+                    refined[:, h * BANK : (h + 1) * BANK], banks[h][:], IDENTITY, bias=bias[:, cb : cb + 1]
                 )
 
             for k in range(PIECES):
                 summed = held.tile([P, S], F32, name=f"summed{cb}_{k}")
                 picked = refined[:].indirect(offsets[:, k * PIECE_COLS : (k + 1) * PIECE_COLS])
                 nc.vector.tensor_tensor(summed[:], picked, samples[cb, k][:], ADD)
-                nc.scalar.dma_start(out[cb * P : (cb + 1) * P, k * S : (k + 1) * S], summed[:])
+                nc.sync.dma_start(out[cb * P : (cb + 1) * P, k * S : (k + 1) * S], summed[:])

@@ -7,6 +7,7 @@ BANK = 512
 HALVES = S // BANK
 PIECES = N // S
 PIECE_COLS = S // 16
+WARMING = 8
 
 FLOPS = 2 * C * C * S
 
@@ -21,7 +22,14 @@ def tile_entityguidedcrossattention_kernel(tc, support, attended, wo, bo, offs, 
     with (
         tc.tile_pool(name="held", bufs=1) as held,
         tc.psum_pool(name="psum", bufs=2) as psum,
+        tc.psum_pool(name="idle", bufs=1) as idle,
     ):
+        zeros = held.tile([P, BANK], BF16, name="zeros")
+        nc.vector.memset(zeros[:], 0.0)
+        unused = idle.tile([P, BANK], F32, name="unused")
+        for turn in range(WARMING):
+            nc.tensor.matmul(unused[:], zeros[:, 0:P], zeros[:], start=True, stop=True)
+
         bias = held.tile([P, BLOCKS], F32, name="bias")
         with nc.allow_non_contiguous_dma(reason="512 bias values, one to a partition"):
             nc.scalar.dma_start(bias[:], bo.rearrange("(b p) o -> p (b o)", p=P))

@@ -6,8 +6,8 @@ BLOCKS = C // P
 BANK = 512
 HALVES = S // BANK
 PIECES = N // S
-PIECE_COLS = S // 16
-WARMING = 8
+TAIL = 256
+WARMING = 4
 
 FLOPS = 2 * C * C * S
 
@@ -19,6 +19,7 @@ IDENTITY = mybir.ActivationFunctionType.Identity
 def tile_entityguidedcrossattention_kernel(tc, support, attended, wo, bo, offs, out):
     nc = tc.nc
     wo_blocks = wo.rearrange("(b p) c -> p b c", p=P)
+    attended_blocks = attended.rearrange("(b p) s -> p b s", p=P)
     with (
         tc.tile_pool(name="held", bufs=1) as held,
         tc.psum_pool(name="psum", bufs=2) as psum,
@@ -41,11 +42,12 @@ def tile_entityguidedcrossattention_kernel(tc, support, attended, wo, bo, offs, 
 
         weights = held.tile([P, BLOCKS, C], BF16, name="weights")
         nc.sync.dma_start(weights[:, :, 0:P], wo_blocks[:, :, 0:P])
-        classes = []
-        for db in range(BLOCKS):
-            a = held.tile([P, S], BF16, name=f"classes{db}")
-            nc.sync.dma_start(a[:], attended[db * P : (db + 1) * P, :])
-            classes.append(a)
+        classes = {}
+        for h in range(HALVES):
+            for pair in range(BLOCKS // 2):
+                a = held.tile([P, 2, BANK], BF16, name=f"classes{h}_{pair}")
+                nc.sync.dma_start(a[:], attended_blocks[:, 2 * pair : 2 * pair + 2, h * BANK : (h + 1) * BANK])
+                classes[h, pair] = a
         offsets = held.tile([P, N // 16], U16, name="offsets")
         nc.sync.dma_start(offsets[:], offs)
         samples = {(0, 0): load_samples(0, 0)}
@@ -57,23 +59,24 @@ def tile_entityguidedcrossattention_kernel(tc, support, attended, wo, bo, offs, 
 
         for cb in range(BLOCKS):
             refined = held.tile([P, S], F32, name=f"refined{cb}")
-            banks = [psum.tile([P, BANK], F32, name=f"bank{h}") for h in range(HALVES)]
-            for db in range(BLOCKS):
-                for h in range(HALVES):
+            for h in range(HALVES):
+                bank = psum.tile([P, BANK], F32, name="bank")
+                for db in range(BLOCKS):
                     nc.tensor.matmul(
-                        banks[h][:],
+                        bank[:],
                         weights[:, db, cb * P : (cb + 1) * P],
-                        classes[db][:, h * BANK : (h + 1) * BANK],
+                        classes[h, db // 2][:, db % 2, :],
                         start=(db == 0),
                         stop=(db == BLOCKS - 1),
                     )
-            for h in range(HALVES):
                 nc.scalar.activation(
-                    refined[:, h * BANK : (h + 1) * BANK], banks[h][:], IDENTITY, bias=bias[:, cb : cb + 1]
+                    refined[:, h * BANK : (h + 1) * BANK], bank[:], IDENTITY, bias=bias[:, cb : cb + 1]
                 )
 
             for k in range(PIECES):
                 summed = held.tile([P, S], F32, name=f"summed{cb}_{k}")
-                picked = refined[:].indirect(offsets[:, k * PIECE_COLS : (k + 1) * PIECE_COLS])
-                nc.vector.tensor_tensor(summed[:], picked, samples[cb, k][:], ADD)
-                nc.sync.dma_start(out[cb * P : (cb + 1) * P, k * S : (k + 1) * S], summed[:])
+                last = cb == BLOCKS - 1 and k == PIECES - 1
+                for lo, hi in [(0, S - TAIL), (S - TAIL, S)] if last else [(0, S)]:
+                    picked = refined[:].indirect(offsets[:, (k * S + lo) // 16 : (k * S + hi) // 16])
+                    nc.vector.tensor_tensor(summed[:, lo:hi], picked, samples[cb, k][:, lo:hi], ADD)
+                    nc.sync.dma_start(out[cb * P : (cb + 1) * P, k * S + lo : k * S + hi], summed[:, lo:hi])

@@ -6,7 +6,7 @@ BLOCKS = C // P
 BANK = 512
 HALVES = S // BANK
 PIECES = N // S
-TAIL = 256
+EDGE = 256
 WARMING = 4
 
 FLOPS = 2 * C * C * S
@@ -35,9 +35,17 @@ def tile_entityguidedcrossattention_kernel(tc, support, attended, wo, bo, offs, 
         with nc.allow_non_contiguous_dma(reason="512 bias values, one to a partition"):
             nc.scalar.dma_start(bias[:], bo.rearrange("(b p) o -> p (b o)", p=P))
 
+        def cuts(cb, k):
+            if (cb, k) == (0, 0):
+                return [(0, EDGE), (EDGE, S)]
+            if (cb, k) == (BLOCKS - 1, PIECES - 1):
+                return [(0, S - EDGE), (S - EDGE, S)]
+            return [(0, S)]
+
         def load_samples(cb, k):
             t = held.tile([P, S], F32, name=f"samples{cb}_{k}")
-            nc.sync.dma_start(t[:], support[cb * P : (cb + 1) * P, k * S : (k + 1) * S])
+            for lo, hi in cuts(cb, k) if (cb, k) == (0, 0) else [(0, S)]:
+                nc.sync.dma_start(t[:, lo:hi], support[cb * P : (cb + 1) * P, k * S + lo : k * S + hi])
             return t
 
         weights = held.tile([P, BLOCKS, C], BF16, name="weights")
@@ -75,8 +83,7 @@ def tile_entityguidedcrossattention_kernel(tc, support, attended, wo, bo, offs, 
 
             for k in range(PIECES):
                 summed = held.tile([P, S], F32, name=f"summed{cb}_{k}")
-                last = cb == BLOCKS - 1 and k == PIECES - 1
-                for lo, hi in [(0, S - TAIL), (S - TAIL, S)] if last else [(0, S)]:
+                for lo, hi in cuts(cb, k):
                     picked = refined[:].indirect(offsets[:, (k * S + lo) // 16 : (k * S + hi) // 16])
                     nc.vector.tensor_tensor(summed[:, lo:hi], picked, samples[cb, k][:, lo:hi], ADD)
                     nc.sync.dma_start(out[cb * P : (cb + 1) * P, k * S + lo : k * S + hi], summed[:, lo:hi])

@@ -7,6 +7,7 @@ BANK = 512
 HALVES = S // BANK
 PIECES = N // S
 EDGE = 256
+LAST = 128
 WARMING = 4
 
 FLOPS = 2 * C * C * S
@@ -39,7 +40,12 @@ def tile_entityguidedcrossattention_kernel(tc, support, attended, wo, bo, offs, 
             if (cb, k) == (0, 0):
                 return [(0, EDGE), (EDGE, S)]
             if (cb, k) == (BLOCKS - 1, PIECES - 1):
-                return [(0, S - EDGE), (S - EDGE, S)]
+                halves = []
+                lo = 0
+                while S - lo > LAST:
+                    halves.append((lo, (lo + S) // 2))
+                    lo = (lo + S) // 2
+                return halves + [(lo, S)]
             return [(0, S)]
 
         def load_samples(cb, k):

@@ -32,9 +32,13 @@ def tile_entityguidedcrossattention_kernel(tc, support, attended, wo, bo, offs, 
         for turn in range(WARMING):
             nc.tensor.matmul(unused[:], zeros[:, 0:P], zeros[:], start=True, stop=True)
 
-        bias = held.tile([P, BLOCKS], F32, name="bias")
+        bo_blocks = bo.rearrange("(b p) o -> p (b o)", p=P)
+        bias_first = held.tile([P, 1], F32, name="bias_first")
+        bias_others = held.tile([P, BLOCKS - 1], F32, name="bias_others")
         with nc.allow_non_contiguous_dma(reason="512 bias values, one to a partition"):
-            nc.scalar.dma_start(bias[:], bo.rearrange("(b p) o -> p (b o)", p=P))
+            nc.scalar.dma_start(bias_first[:], bo_blocks[:, 0:1])
+            nc.gpsimd.dma_start(bias_others[:], bo_blocks[:, 1:BLOCKS])
+        bias = [bias_first[:, 0:1]] + [bias_others[:, cb - 1 : cb] for cb in range(1, BLOCKS)]
 
         def cuts(cb, k):
             if (cb, k) == (0, 0):
@@ -60,32 +64,44 @@ def tile_entityguidedcrossattention_kernel(tc, support, attended, wo, bo, offs, 
         for h in range(HALVES):
             for pair in range(BLOCKS // 2):
                 a = held.tile([P, 2, BANK], BF16, name=f"classes{h}_{pair}")
-                nc.sync.dma_start(a[:], attended_blocks[:, 2 * pair : 2 * pair + 2, h * BANK : (h + 1) * BANK])
+                last = (h, pair) == (HALVES - 1, BLOCKS // 2 - 1)
+                for lo, hi in [(0, 1), (1, 2)] if last else [(0, 2)]:
+                    nc.sync.dma_start(
+                        a[:, lo:hi, :], attended_blocks[:, 2 * pair + lo : 2 * pair + hi, h * BANK : (h + 1) * BANK]
+                    )
                 classes[h, pair] = a
         offsets = held.tile([P, N // 16], U16, name="offsets")
         nc.sync.dma_start(offsets[:], offs)
-        samples = {(0, 0): load_samples(0, 0)}
-        nc.sync.dma_start(weights[:, :, P:C], wo_blocks[:, :, P:C])
+        samples = {}
         for cb in range(BLOCKS):
             for k in range(PIECES):
-                if (cb, k) != (0, 0):
-                    samples[cb, k] = load_samples(cb, k)
+                if k == PIECES - 1 and cb + 1 < BLOCKS:
+                    nc.sync.dma_start(
+                        weights[:, :, (cb + 1) * P : (cb + 2) * P], wo_blocks[:, :, (cb + 1) * P : (cb + 2) * P]
+                    )
+                samples[cb, k] = load_samples(cb, k)
 
         for cb in range(BLOCKS):
             refined = held.tile([P, S], F32, name=f"refined{cb}")
             for h in range(HALVES):
-                bank = psum.tile([P, BANK], F32, name="bank")
+                parts = 2 if (cb, h) == (0, HALVES - 1) else 1
+                width = BANK // parts
+                banks = [psum.tile([P, BANK], F32, name=f"bank{q}") for q in range(parts)]
                 for db in range(BLOCKS):
-                    nc.tensor.matmul(
-                        bank[:],
-                        weights[:, db, cb * P : (cb + 1) * P],
-                        classes[h, db // 2][:, db % 2, :],
-                        start=(db == 0),
-                        stop=(db == BLOCKS - 1),
-                    )
-                nc.scalar.activation(
-                    refined[:, h * BANK : (h + 1) * BANK], bank[:], IDENTITY, bias=bias[:, cb : cb + 1]
-                )
+                    for q in range(parts):
+                        nc.tensor.matmul(
+                            banks[q][:, 0:width],
+                            weights[:, db, cb * P : (cb + 1) * P],
+                            classes[h, db // 2][:, db % 2, q * width : (q + 1) * width],
+                            start=(db == 0),
+                            stop=(db == BLOCKS - 1),
+                        )
+                for q in range(parts):
+                    columns = refined[:, h * BANK + q * width : h * BANK + (q + 1) * width]
+                    if q == 0:
+                        nc.scalar.activation(columns, banks[q][:, 0:width], IDENTITY, bias=bias[cb])
+                    else:
+                        nc.vector.tensor_scalar_add(columns, banks[q][:, 0:width], bias[cb])
 
             for k in range(PIECES):
                 summed = held.tile([P, S], F32, name=f"summed{cb}_{k}")

@@ -9,6 +9,7 @@ PIECES = N // S
 EDGE = 256
 LAST = 128
 WARMING = 4
+ROW = 256
 
 FLOPS = 2 * C * C * S
 
@@ -53,24 +54,24 @@ def tile_entityguidedcrossattention_kernel(tc, support, attended, wo, bo, offs, 
             return [(0, S)]
 
         def load_samples(cb, k):
-            t = held.tile([P, S], F32, name=f"samples{cb}_{k}")
+            t = held.tile([P, S], F32, name=f"samples{cb}_{k}", align_bytes=ROW)
             for lo, hi in cuts(cb, k) if (cb, k) == (0, 0) else [(0, S)]:
                 nc.sync.dma_start(t[:, lo:hi], support[cb * P : (cb + 1) * P, k * S + lo : k * S + hi])
             return t
 
-        weights = held.tile([P, BLOCKS, C], BF16, name="weights")
+        weights = held.tile([P, BLOCKS, C], BF16, name="weights", align_bytes=ROW)
         nc.sync.dma_start(weights[:, :, 0:P], wo_blocks[:, :, 0:P])
         classes = {}
         for h in range(HALVES):
             for pair in range(BLOCKS // 2):
-                a = held.tile([P, 2, BANK], BF16, name=f"classes{h}_{pair}")
+                a = held.tile([P, 2, BANK], BF16, name=f"classes{h}_{pair}", align_bytes=ROW)
                 last = (h, pair) == (HALVES - 1, BLOCKS // 2 - 1)
                 for lo, hi in [(0, 1), (1, 2)] if last else [(0, 2)]:
                     nc.sync.dma_start(
                         a[:, lo:hi, :], attended_blocks[:, 2 * pair + lo : 2 * pair + hi, h * BANK : (h + 1) * BANK]
                     )
                 classes[h, pair] = a
-        offsets = held.tile([P, N // 16], U16, name="offsets")
+        offsets = held.tile([P, N // 16], U16, name="offsets", align_bytes=ROW)
         nc.sync.dma_start(offsets[:], offs)
         samples = {}
         for cb in range(BLOCKS):
@@ -104,7 +105,7 @@ def tile_entityguidedcrossattention_kernel(tc, support, attended, wo, bo, offs, 
                         nc.vector.tensor_scalar_add(columns, banks[q][:, 0:width], bias[cb])
 
             for k in range(PIECES):
-                summed = held.tile([P, S], F32, name=f"summed{cb}_{k}")
+                summed = held.tile([P, S], F32, name=f"summed{cb}_{k}", align_bytes=ROW)
                 for lo, hi in cuts(cb, k):
                     picked = refined[:].indirect(offsets[:, (k * S + lo) // 16 : (k * S + hi) // 16])
                     nc.vector.tensor_tensor(summed[:, lo:hi], picked, samples[cb, k][:, lo:hi], ADD)

@@ -36,9 +36,8 @@ def tile_entityguidedcrossattention_kernel(tc, support, attended, wo, bo, offs, 
         bo_blocks = bo.rearrange("(b p) o -> p (b o)", p=P)
         bias_first = held.tile([P, 1], F32, name="bias_first")
         bias_others = held.tile([P, BLOCKS - 1], F32, name="bias_others")
-        with nc.allow_non_contiguous_dma(reason="512 bias values, one to a partition"):
+        with nc.allow_non_contiguous_dma(reason="128 bias values, one to a partition"):
             nc.scalar.dma_start(bias_first[:], bo_blocks[:, 0:1])
-            nc.gpsimd.dma_start(bias_others[:], bo_blocks[:, 1:BLOCKS])
         bias = [bias_first[:, 0:1]] + [bias_others[:, cb - 1 : cb] for cb in range(1, BLOCKS)]
 
         def cuts(cb, k):
@@ -65,17 +64,16 @@ def tile_entityguidedcrossattention_kernel(tc, support, attended, wo, bo, offs, 
         for h in range(HALVES):
             for pair in range(BLOCKS // 2):
                 a = held.tile([P, 2, BANK], BF16, name=f"classes{h}_{pair}", align_bytes=ROW)
-                last = (h, pair) == (HALVES - 1, BLOCKS // 2 - 1)
-                for lo, hi in [(0, 1), (1, 2)] if last else [(0, 2)]:
-                    nc.sync.dma_start(
-                        a[:, lo:hi, :], attended_blocks[:, 2 * pair + lo : 2 * pair + hi, h * BANK : (h + 1) * BANK]
-                    )
+                nc.sync.dma_start(a[:], attended_blocks[:, 2 * pair : 2 * pair + 2, h * BANK : (h + 1) * BANK])
                 classes[h, pair] = a
         offsets = held.tile([P, N // 16], U16, name="offsets", align_bytes=ROW)
         nc.sync.dma_start(offsets[:], offs)
         samples = {}
         for cb in range(BLOCKS):
             for k in range(PIECES):
+                if k == PIECES - 1 and cb == 0:
+                    with nc.allow_non_contiguous_dma(reason="384 bias values, one to a partition"):
+                        nc.sync.dma_start(bias_others[:], bo_blocks[:, 1:BLOCKS])
                 if k == PIECES - 1 and cb + 1 < BLOCKS:
                     nc.sync.dma_start(
                         weights[:, :, (cb + 1) * P : (cb + 2) * P], wo_blocks[:, :, (cb + 1) * P : (cb + 2) * P]

@@ -6,7 +6,6 @@ BLOCKS = C // P
 BANK = 512
 HALVES = S // BANK
 PIECES = N // S
-EDGE = 256
 LAST = 128
 WARMING = 4
 ROW = 256
@@ -41,8 +40,6 @@ def tile_entityguidedcrossattention_kernel(tc, support, attended, wo, bo, offs, 
         bias = [bias_first[:, 0:1]] + [bias_others[:, cb - 1 : cb] for cb in range(1, BLOCKS)]
 
         def cuts(cb, k):
-            if (cb, k) == (0, 0):
-                return [(0, EDGE), (EDGE, S)]
             if (cb, k) == (BLOCKS - 1, PIECES - 1):
                 halves = []
                 lo = 0
@@ -54,8 +51,7 @@ def tile_entityguidedcrossattention_kernel(tc, support, attended, wo, bo, offs, 
 
         def load_samples(cb, k):
             t = held.tile([P, S], F32, name=f"samples{cb}_{k}", align_bytes=ROW)
-            for lo, hi in cuts(cb, k) if (cb, k) == (0, 0) else [(0, S)]:
-                nc.sync.dma_start(t[:, lo:hi], support[cb * P : (cb + 1) * P, k * S + lo : k * S + hi])
+            nc.sync.dma_start(t[:], support[cb * P : (cb + 1) * P, k * S : (k + 1) * S])
             return t
 
         weights = held.tile([P, BLOCKS, C], BF16, name="weights", align_bytes=ROW)
@@ -64,7 +60,11 @@ def tile_entityguidedcrossattention_kernel(tc, support, attended, wo, bo, offs, 
         for h in range(HALVES):
             for pair in range(BLOCKS // 2):
                 a = held.tile([P, 2, BANK], BF16, name=f"classes{h}_{pair}", align_bytes=ROW)
-                nc.sync.dma_start(a[:], attended_blocks[:, 2 * pair : 2 * pair + 2, h * BANK : (h + 1) * BANK])
+                ends = (h, pair) in [(0, 0), (HALVES - 1, BLOCKS // 2 - 1)]
+                for lo, hi in [(0, 1), (1, 2)] if ends else [(0, 2)]:
+                    nc.sync.dma_start(
+                        a[:, lo:hi, :], attended_blocks[:, 2 * pair + lo : 2 * pair + hi, h * BANK : (h + 1) * BANK]
+                    )
                 classes[h, pair] = a
         offsets = held.tile([P, N // 16], U16, name="offsets", align_bytes=ROW)
         nc.sync.dma_start(offsets[:], offs)

@@ -32,11 +32,15 @@ def tile_entityguidedcrossattention_kernel(tc, support, attended, wo, bo, offs, 
         for turn in range(WARMING):
             nc.tensor.matmul(unused[:], zeros[:, 0:P], zeros[:], start=True, stop=True)
 
+        weights = held.tile([P, BLOCKS, C], BF16, name="weights", align_bytes=ROW)
+        nc.scalar.dma_start(weights[:, :, 0:P], wo_blocks[:, :, 0:P])
+
+        table_load = held.tile([P, 1], F32, name="table_load")
+        nc.scalar.activation(table_load[:], zeros[:, 0:1], IDENTITY)
+
         bo_blocks = bo.rearrange("(b p) o -> p (b o)", p=P)
         bias_first = held.tile([P, 1], F32, name="bias_first")
         bias_others = held.tile([P, BLOCKS - 1], F32, name="bias_others")
-        with nc.allow_non_contiguous_dma(reason="128 bias values, one to a partition"):
-            nc.scalar.dma_start(bias_first[:], bo_blocks[:, 0:1])
         bias = [bias_first[:, 0:1]] + [bias_others[:, cb - 1 : cb] for cb in range(1, BLOCKS)]
 
         def cuts(cb, k):
@@ -54,8 +58,6 @@ def tile_entityguidedcrossattention_kernel(tc, support, attended, wo, bo, offs, 
             nc.sync.dma_start(t[:], support[cb * P : (cb + 1) * P, k * S : (k + 1) * S])
             return t
 
-        weights = held.tile([P, BLOCKS, C], BF16, name="weights", align_bytes=ROW)
-        nc.sync.dma_start(weights[:, :, 0:P], wo_blocks[:, :, 0:P])
         classes = {}
         for h in range(HALVES):
             for pair in range(BLOCKS // 2):
@@ -66,6 +68,8 @@ def tile_entityguidedcrossattention_kernel(tc, support, attended, wo, bo, offs, 
                         a[:, lo:hi, :], attended_blocks[:, 2 * pair + lo : 2 * pair + hi, h * BANK : (h + 1) * BANK]
                     )
                 classes[h, pair] = a
+        with nc.allow_non_contiguous_dma(reason="128 bias values, one to a partition"):
+            nc.sync.dma_start(bias_first[:], bo_blocks[:, 0:1])
         offsets = held.tile([P, N // 16], U16, name="offsets", align_bytes=ROW)
         nc.sync.dma_start(offsets[:], offs)
         samples = {}

@@ -59,12 +59,14 @@ def tile_entityguidedcrossattention_kernel(tc, support, attended, wo, bo, offs, 
             return t
 
         classes = {}
+        queue, other_queue = nc.scalar, nc.sync
         for h in range(HALVES):
             for pair in range(BLOCKS // 2):
                 a = held.tile([P, 2, BANK], BF16, name=f"classes{h}_{pair}", align_bytes=ROW)
                 ends = (h, pair) in [(0, 0), (HALVES - 1, BLOCKS // 2 - 1)]
                 for lo, hi in [(0, 1), (1, 2)] if ends else [(0, 2)]:
-                    nc.sync.dma_start(
+                    queue, other_queue = other_queue, queue
+                    queue.dma_start(
                         a[:, lo:hi, :], attended_blocks[:, 2 * pair + lo : 2 * pair + hi, h * BANK : (h + 1) * BANK]
                     )
                 classes[h, pair] = a

@@ -33,7 +33,9 @@ def tile_entityguidedcrossattention_kernel(tc, support, attended, wo, bo, offs, 
             nc.tensor.matmul(unused[:], zeros[:, 0:P], zeros[:], start=True, stop=True)
 
         weights = held.tile([P, BLOCKS, C], BF16, name="weights", align_bytes=ROW)
-        nc.scalar.dma_start(weights[:, :, 0:P], wo_blocks[:, :, 0:P])
+        half = BLOCKS // 2
+        nc.scalar.dma_start(weights[:, 0:half, 0:P], wo_blocks[:, 0:half, 0:P])
+        nc.sync.dma_start(weights[:, half:BLOCKS, 0:P], wo_blocks[:, half:BLOCKS, 0:P])
 
         table_load = held.tile([P, 1], F32, name="table_load")
         nc.scalar.activation(table_load[:], zeros[:, 0:1], IDENTITY)
@@ -75,15 +77,15 @@ def tile_entityguidedcrossattention_kernel(tc, support, attended, wo, bo, offs, 
         offsets = held.tile([P, N // 16], U16, name="offsets", align_bytes=ROW)
         nc.sync.dma_start(offsets[:], offs)
         samples = {}
+        next_weights = {0: (1, 2), 1: (2, BLOCKS)}
         for cb in range(BLOCKS):
             for k in range(PIECES):
                 if k == PIECES - 1 and cb == 0:
                     with nc.allow_non_contiguous_dma(reason="384 bias values, one to a partition"):
                         nc.sync.dma_start(bias_others[:], bo_blocks[:, 1:BLOCKS])
-                if k == PIECES - 1 and cb + 1 < BLOCKS:
-                    nc.sync.dma_start(
-                        weights[:, :, (cb + 1) * P : (cb + 2) * P], wo_blocks[:, :, (cb + 1) * P : (cb + 2) * P]
-                    )
+                if k == PIECES - 1 and cb in next_weights:
+                    lo, hi = next_weights[cb]
+                    nc.sync.dma_start(weights[:, :, lo * P : hi * P], wo_blocks[:, :, lo * P : hi * P])
                 samples[cb, k] = load_samples(cb, k)
 
         for cb in range(BLOCKS):

import concourse.mybir as mybir

P = 128
C, S, N = 512, 1024, 2048
BLOCKS = C // P
BANK = 512
HALVES = S // BANK
PIECES = N // S
LAST = 128
WARMING = 4
ROW = 256

FLOPS = 2 * C * C * S

BF16, F32, U16 = mybir.dt.bfloat16, mybir.dt.float32, mybir.dt.uint16
ADD = mybir.AluOpType.add
IDENTITY = mybir.ActivationFunctionType.Identity


def tile_entityguidedcrossattention_kernel(tc, support, attended, wo, bo, offs, out):
    nc = tc.nc
    wo_blocks = wo.rearrange("(b p) c -> p b c", p=P)
    attended_blocks = attended.rearrange("(b p) s -> p b s", p=P)
    with (
        tc.tile_pool(name="held", bufs=1) as held,
        tc.psum_pool(name="psum", bufs=2) as psum,
        tc.psum_pool(name="idle", bufs=1) as idle,
    ):
        zeros = held.tile([P, BANK], BF16, name="zeros")
        nc.vector.memset(zeros[:], 0.0)
        unused = idle.tile([P, BANK], F32, name="unused")
        for turn in range(WARMING):
            nc.tensor.matmul(unused[:], zeros[:, 0:P], zeros[:], start=True, stop=True)

        weights = held.tile([P, BLOCKS, C], BF16, name="weights", align_bytes=ROW)
        half = BLOCKS // 2
        nc.scalar.dma_start(weights[:, 0:half, 0:P], wo_blocks[:, 0:half, 0:P])
        nc.sync.dma_start(weights[:, half:BLOCKS, 0:P], wo_blocks[:, half:BLOCKS, 0:P])

        table_load = held.tile([P, 1], F32, name="table_load")
        nc.scalar.activation(table_load[:], zeros[:, 0:1], IDENTITY)

        bo_blocks = bo.rearrange("(b p) o -> p (b o)", p=P)
        bias_first = held.tile([P, 1], F32, name="bias_first")
        bias_others = held.tile([P, BLOCKS - 1], F32, name="bias_others")
        bias = [bias_first[:, 0:1]] + [bias_others[:, cb - 1 : cb] for cb in range(1, BLOCKS)]

        def cuts(cb, k):
            if (cb, k) == (BLOCKS - 1, PIECES - 1):
                halves = []
                lo = 0
                while S - lo > LAST:
                    halves.append((lo, (lo + S) // 2))
                    lo = (lo + S) // 2
                return halves + [(lo, S)]
            return [(0, S)]

        def load_samples(cb, k):
            t = held.tile([P, S], F32, name=f"samples{cb}_{k}", align_bytes=ROW)
            nc.sync.dma_start(t[:], support[cb * P : (cb + 1) * P, k * S : (k + 1) * S])
            return t

        classes = {}
        queue, other_queue = nc.scalar, nc.sync
        for h in range(HALVES):
            for pair in range(BLOCKS // 2):
                a = held.tile([P, 2, BANK], BF16, name=f"classes{h}_{pair}", align_bytes=ROW)
                ends = (h, pair) in [(0, 0), (HALVES - 1, BLOCKS // 2 - 1)]
                for lo, hi in [(0, 1), (1, 2)] if ends else [(0, 2)]:
                    queue, other_queue = other_queue, queue
                    queue.dma_start(
                        a[:, lo:hi, :], attended_blocks[:, 2 * pair + lo : 2 * pair + hi, h * BANK : (h + 1) * BANK]
                    )
                classes[h, pair] = a
        with nc.allow_non_contiguous_dma(reason="128 bias values, one to a partition"):
            nc.sync.dma_start(bias_first[:], bo_blocks[:, 0:1])
        offsets = held.tile([P, N // 16], U16, name="offsets", align_bytes=ROW)
        nc.sync.dma_start(offsets[:], offs)
        samples = {}
        next_weights = {0: (1, 2), 1: (2, BLOCKS)}
        for cb in range(BLOCKS):
            for k in range(PIECES):
                if k == PIECES - 1 and cb == 0:
                    with nc.allow_non_contiguous_dma(reason="384 bias values, one to a partition"):
                        nc.sync.dma_start(bias_others[:], bo_blocks[:, 1:BLOCKS])
                if k == PIECES - 1 and cb in next_weights:
                    lo, hi = next_weights[cb]
                    nc.sync.dma_start(weights[:, :, lo * P : hi * P], wo_blocks[:, :, lo * P : hi * P])
                samples[cb, k] = load_samples(cb, k)

        for cb in range(BLOCKS):
            refined = held.tile([P, S], F32, name=f"refined{cb}")
            for h in range(HALVES):
                parts = 2 if (cb, h) == (0, HALVES - 1) else 1
                width = BANK // parts
                banks = [psum.tile([P, BANK], F32, name=f"bank{q}") for q in range(parts)]
                for db in range(BLOCKS):
                    for q in range(parts):
                        nc.tensor.matmul(
                            banks[q][:, 0:width],
                            weights[:, db, cb * P : (cb + 1) * P],
                            classes[h, db // 2][:, db % 2, q * width : (q + 1) * width],
                            start=(db == 0),
                            stop=(db == BLOCKS - 1),
                        )
                for q in range(parts):
                    columns = refined[:, h * BANK + q * width : h * BANK + (q + 1) * width]
                    if q == 0:
                        nc.scalar.activation(columns, banks[q][:, 0:width], IDENTITY, bias=bias[cb])
                    else:
                        nc.vector.tensor_scalar_add(columns, banks[q][:, 0:width], bias[cb])

            for k in range(PIECES):
                summed = held.tile([P, S], F32, name=f"summed{cb}_{k}", align_bytes=ROW)
                for lo, hi in cuts(cb, k):
                    picked = refined[:].indirect(offsets[:, (k * S + lo) // 16 : (k * S + hi) // 16])
                    nc.vector.tensor_tensor(summed[:, lo:hi], picked, samples[cb, k][:, lo:hi], ADD)
                    nc.sync.dma_start(out[cb * P : (cb + 1) * P, k * S + lo : k * S + hi], summed[:, lo:hi])
